import numpy as np
import ml_dtypes


def mxq(x, axis, fmt="e4m3"):
    dtype, down = {"e4m3": (ml_dtypes.float8_e4m3fn, 7), "e5m2": (ml_dtypes.float8_e5m2, 14)}[fmt]
    v = np.moveaxis(np.asarray(x, np.float32).astype(ml_dtypes.bfloat16).astype(np.float64), axis, -1)
    blocks = v.reshape(v.shape[:-1] + (-1, 32))
    amax = np.abs(blocks).max(-1, keepdims=True)
    byte = np.maximum(np.where(amax > 0, np.frexp(amax)[1] - 1 + 127, 0) - down, 1)
    scale = np.exp2(byte - 127.0)
    codes = (blocks / scale).astype(np.float32).astype(dtype).astype(np.float64)
    return np.moveaxis((codes * scale).reshape(v.shape), -1, axis)


WIDE = False


def mx_kscale(k):
    if not WIDE:
        return np.ones(k)
    levels = np.array([10, -10, 5, -5, 0])
    a = np.random.permutation(np.resize(levels, k // 512 * 4)).reshape(k // 512, 4)
    idx = np.arange(k)
    return np.exp2(a[idx // 512, idx % 128 // 32])


BF16 = ml_dtypes.bfloat16


def bf(x):
    return np.asarray(x, np.float32).astype(BF16)


def f64(x):
    return np.asarray(x).astype(np.float64)


E2M1 = np.array([0.0, 0.5, 1.0, 1.5, 2.0, 3.0, 4.0, 6.0, -0.0, -0.5, -1.0, -1.5, -2.0, -3.0, -4.0, -6.0])


def pack_weight(w, fmt):
    k, n = w.shape
    w = f64(bf(w)).reshape(k // 32, 32, n)
    amax = np.abs(w).max(1)
    if fmt == "e4m3":
        byte = np.frexp(amax)[1] - 1 + 127 - 7
    else:
        mant, ex = np.frexp(amax / 6.0)
        byte = np.where(mant > 0.5, ex, ex - 1) + 127
    byte = np.clip(np.where(amax > 0, byte, 1), 1, 254)
    scaled = (w * np.exp2(127.0 - byte)[:, None, :]).reshape(k, n).astype(np.float32)
    by_word = np.ascontiguousarray(scaled.reshape(k // 512, 128, 4, n).transpose(0, 1, 3, 2))
    if fmt == "e4m3":
        words = by_word.astype(ml_dtypes.float8_e4m3fn).view(np.uint8)
    else:
        c = by_word.astype(ml_dtypes.float4_e2m1fn).view(np.uint8) & 0xF
        words = c[..., 0::2] | (c[..., 1::2] << 4)
    return np.ascontiguousarray(words), np.ascontiguousarray(byte.astype(np.uint8).reshape(k // 512, 16, n))


def unpack_weight(words, scales, fmt):
    g, p, n, _ = words.shape
    if fmt == "e4m3":
        vals = np.ascontiguousarray(words).view(ml_dtypes.float8_e4m3fn).astype(np.float64)
    else:
        nib = np.empty((g, p, n, 4), np.uint8)
        nib[..., 0::2] = words & 0xF
        nib[..., 1::2] = words >> 4
        vals = E2M1[nib]
    vals = vals * np.repeat(np.exp2(scales.astype(np.float64) - 127.0), 8, axis=1)[..., None]
    return vals.transpose(0, 1, 3, 2).reshape(g * 512, n)

def pack4(w):
    words, scales = pack_weight(w, "e2m1")
    return words.reshape(words.shape[0], 128, -1), scales


def unpack4(words, scales):
    return unpack_weight(words.reshape(words.shape[0], 128, -1, 2), scales, "e2m1")


H, D_CONTENT, D_POS, D_K, D_V, B, L = 8, 384, 128, 128, 128, 4, 128
D_MODEL = D_CONTENT + D_POS
T = B * L
DV1 = D_V // 2
KP = H * DV1
EPS = 1e-3


def setup_inputs():
    s1, s2 = mx_kscale(KP), mx_kscale(KP)
    sc = np.concatenate([s1.reshape(H, DV1), s2.reshape(H, DV1)], axis=1)
    attn_out = bf(np.random.standard_normal((H, B, L, D_V)) * 0.4 * sc[:, None, None, :])
    inp = bf(np.random.standard_normal((T, D_MODEL)) * 0.05 + np.random.standard_normal((T, 1)) * 0.03)
    w_proj1_words, w_proj1_scales = pack4(np.random.standard_normal((KP, D_CONTENT)) * 0.1 / np.sqrt(KP) / s1[:, None])
    w_proj2_words, w_proj2_scales = pack4(np.random.standard_normal((KP, D_POS)) * 0.1 / np.sqrt(KP) / s2[:, None])
    ln_a = bf(1.0 + 0.1 * np.random.standard_normal(D_MODEL))
    ln_b = bf(0.1 * np.random.standard_normal(D_MODEL))
    return {
        "attn_out": attn_out,
        "inp": inp,
        "w_proj1_words": w_proj1_words,
        "w_proj1_scales": w_proj1_scales,
        "w_proj2_words": w_proj2_words,
        "w_proj2_scales": w_proj2_scales,
        "ln_a": ln_a,
        "ln_b": ln_b,
    }


def reference(attn_out, inp, w_proj1_words, w_proj1_scales, w_proj2_words, w_proj2_scales, ln_a, ln_b):
    o = f64(attn_out).reshape(H, T, D_V).transpose(1, 0, 2)
    o1 = o[:, :, :DV1].reshape(T, KP)
    o2 = o[:, :, DV1:].reshape(T, KP)
    y1 = mxq(o1, 1, "e4m3") @ unpack4(w_proj1_words, w_proj1_scales)
    y2 = mxq(o2, 1, "e4m3") @ unpack4(w_proj2_words, w_proj2_scales)
    z = np.concatenate([y1, y2], -1) + f64(inp)
    mu = np.mean(z, axis=-1, keepdims=True)
    sigma = np.std(z, axis=-1, keepdims=True, ddof=1)
    ln = (z - mu) / (sigma + EPS)
    return ln * f64(ln_a) + f64(ln_b)

@@ -1,0 +1,167 @@
+from contextlib import ExitStack
+
+import concourse.mybir as mybir
+from concourse.masks import make_identity
+
+F32 = mybir.dt.float32
+BF16 = mybir.dt.bfloat16
+I32 = mybir.dt.int32
+U32 = mybir.dt.uint32
+U8 = mybir.dt.uint8
+FP8X4 = mybir.dt.float8_e4m3fn_x4
+FP4X4 = mybir.dt.float4_e2m1fn_x4
+ALU = mybir.AluOpType
+ACT = mybir.ActivationFunctionType
+
+P = 128
+HEADS = 8
+HALF = 64
+SENTENCES = 4
+K = HEADS * HALF
+D_CONTENT = 384
+D_MODEL = 512
+N_GROUP = 128
+EPS = 1e-3
+
+FLOPS = 2 * SENTENCES * P * K * D_MODEL
+
+
+def load_scale_rows(nc, plane, scale_rows):
+    for a in range(4):
+        nc.sync.dma_start(
+            out=plane[32 * a : 32 * a + 4, :].bitcast(I32),
+            in_=scale_rows[4 * a : 4 * a + 4, :].bitcast(I32),
+        )
+
+
+def tile_multiheadattention_pa_s_kernel(
+    tc,
+    attn_out,
+    inp,
+    w_proj1_words,
+    w_proj1_scales,
+    w_proj2_words,
+    w_proj2_scales,
+    ln_a,
+    ln_b,
+    out,
+):
+    nc = tc.nc
+    with ExitStack() as ctx:
+        const = ctx.enter_context(tc.tile_pool(name="const", bufs=1))
+        feature_pool = ctx.enter_context(tc.tile_pool(name="features", bufs=2 * SENTENCES))
+        operand_pool = ctx.enter_context(tc.tile_pool(name="operands", bufs=4))
+        row_pool = ctx.enter_context(tc.tile_pool(name="rows", bufs=3))
+        stat_pool = ctx.enter_context(tc.tile_pool(name="stats", bufs=4))
+        transposed_pool = ctx.enter_context(tc.psum_pool(name="transposed", bufs=4))
+        product_pool = ctx.enter_context(tc.psum_pool(name="product", bufs=3))
+
+        w_words = const.tile([P, 2 * D_MODEL], U8, align_bytes=64)
+        w_scales = const.tile([P, D_MODEL], U8, align_bytes=64)
+        nc.vector.memset(w_scales[:].bitcast(I32), 0)
+
+        features = {}
+
+        def load_features(b, half):
+            x = feature_pool.tile([P, HEADS, HALF], BF16)
+            nc.sync.dma_start(
+                out=x[:],
+                in_=attn_out[:, b, :, half * HALF : (half + 1) * HALF].rearrange("h l j -> l h j"),
+            )
+            features[(b, half)] = x
+
+        load_features(0, 0)
+        load_scale_rows(nc, w_scales[:, :D_CONTENT], w_proj1_scales[0])
+        nc.sync.dma_start(out=w_words[:, : 2 * D_CONTENT].bitcast(I32), in_=w_proj1_words[0].bitcast(I32))
+        load_features(0, 1)
+        nc.sync.dma_start(out=w_words[:, 2 * D_CONTENT :].bitcast(I32), in_=w_proj2_words[0].bitcast(I32))
+        load_scale_rows(nc, w_scales[:, D_CONTENT:], w_proj2_scales[0])
+        for b in range(1, SENTENCES):
+            for half in range(2):
+                load_features(b, half)
+
+        residual = const.tile([P, SENTENCES, D_MODEL], BF16)
+        nc.gpsimd.dma_start(out=residual[:], in_=inp.rearrange("(b l) c -> l b c", l=P))
+
+        identity = const.tile([P, P], F32)
+        make_identity(nc, identity[:])
+
+        gain = const.tile([P, D_MODEL], BF16)
+        bias = const.tile([P, D_MODEL], BF16)
+        nc.gpsimd.dma_start(out=gain[:], in_=ln_a.partition_broadcast(P))
+        nc.gpsimd.dma_start(out=bias[:], in_=ln_b.partition_broadcast(P))
+
+        one = const.tile([P, 1], F32)
+        nc.vector.memset(one[:], 1.0)
+        nc.scalar.activation(out=one[:], in_=one[:], func=ACT.Sqrt)
+
+        def project(b):
+            z_psum = product_pool.tile([P, D_MODEL], F32)
+            for half in range(2):
+                x_words = features[(b, half)][:].rearrange("l h j -> l (h j)").bitcast(F32)
+                transposed = transposed_pool.tile([P, 2, P], F32)
+                for u in range(2):
+                    nc.tensor.transpose(transposed[:, u, :], x_words[:, u : K // 2 : 2], identity[:])
+                grouped = operand_pool.tile([P, P, 4], BF16, align_bytes=64)
+                nc.scalar.copy(out=grouped[:].bitcast(F32), in_=transposed[:].rearrange("p u l -> p l u"))
+                codes = operand_pool.tile([P, P], U32, align_bytes=64)
+                scales = operand_pool.tile([P, P], U8, align_bytes=64)
+                nc.vector.quantize_mx(
+                    out=codes[:].bitcast(FP8X4),
+                    scales=scales[:],
+                    in_=grouped[:].rearrange("p l t -> p (l t)"),
+                )
+                first, last = (0, D_CONTENT) if half == 0 else (D_CONTENT, D_MODEL)
+                for n in range(first, last, N_GROUP):
+                    nc.tensor.matmul_mx(
+                        out=z_psum[:, n : n + N_GROUP],
+                        lhsT=codes[:].bitcast(FP8X4),
+                        lhsT_scale=scales[:],
+                        rhs=w_words[:, 2 * n : 2 * (n + N_GROUP)].bitcast(FP4X4),
+                        rhs_scale=w_scales[:, n : n + N_GROUP],
+                        start=True,
+                        stop=True,
+                    )
+            return z_psum
+
+        def normalise(b, z_psum):
+            z = row_pool.tile([P, D_MODEL], F32)
+            row_sum = stat_pool.tile([P, 1], F32)
+            nc.vector.scalar_tensor_tensor(
+                out=z[:],
+                in0=z_psum[:],
+                scalar=1.0,
+                in1=residual[:, b, :],
+                op0=ALU.mult,
+                op1=ALU.add,
+                accum_out=row_sum[:],
+            )
+            neg_mean = stat_pool.tile([P, 1], F32)
+            nc.vector.tensor_scalar(
+                out=neg_mean[:], in0=row_sum[:], scalar1=-1.0 / D_MODEL, scalar2=None, op0=ALU.mult
+            )
+            squares = row_pool.tile([P, D_MODEL], BF16)
+            sum_squares = stat_pool.tile([P, 1], F32)
+            nc.scalar.activation(
+                out=squares[:], in_=z[:], func=ACT.Square, bias=neg_mean[:], accum_out=sum_squares[:]
+            )
+            sigma = stat_pool.tile([P, 1], F32)
+            nc.scalar.activation(out=sigma[:], in_=sum_squares[:], func=ACT.Sqrt, scale=1.0 / (D_MODEL - 1))
+            centred = row_pool.tile([P, D_MODEL], F32)
+            nc.vector.scalar_tensor_tensor(
+                out=centred[:], in0=z[:], scalar=neg_mean[:], in1=gain[:], op0=ALU.add, op1=ALU.mult
+            )
+            inverse = stat_pool.tile([P, 1], F32)
+            nc.vector.tensor_scalar(out=inverse[:], in0=sigma[:], scalar1=EPS, scalar2=None, op0=ALU.add)
+            nc.vector.reciprocal(out=inverse[:], in_=inverse[:])
+            result = row_pool.tile([P, D_MODEL], F32)
+            nc.vector.scalar_tensor_tensor(
+                out=result[:], in0=centred[:], scalar=inverse[:], in1=bias[:], op0=ALU.mult, op1=ALU.add
+            )
+            nc.sync.dma_start(out=out[b * P : (b + 1) * P, :], in_=result[:])
+
+        products = [project(0)]
+        for b in range(SENTENCES):
+            if b + 1 < SENTENCES:
+                products.append(project(b + 1))
+            normalise(b, products[b])

@@ -21,6 +21,7 @@ K = HEADS * HALF
 D_CONTENT = 384
 D_MODEL = 512
 N_GROUP = 128
+VECTOR_ROWS = D_MODEL // P
 EPS = 1e-3
 
 FLOPS = 2 * SENTENCES * P * K * D_MODEL
@@ -53,14 +54,22 @@ def tile_multiheadattention_pa_s_kernel(
         operand_pool = ctx.enter_context(tc.tile_pool(name="operands", bufs=4))
         row_pool = ctx.enter_context(tc.tile_pool(name="rows", bufs=3))
         stat_pool = ctx.enter_context(tc.tile_pool(name="stats", bufs=4))
-        transposed_pool = ctx.enter_context(tc.psum_pool(name="transposed", bufs=4))
+        transposed_pool = ctx.enter_context(tc.psum_pool(name="transposed", bufs=3))
         product_pool = ctx.enter_context(tc.psum_pool(name="product", bufs=3))
+        spread_pool = ctx.enter_context(tc.psum_pool(name="spread", bufs=1))
 
         w_words = const.tile([P, 2 * D_MODEL], U8, align_bytes=64)
         w_scales = const.tile([P, D_MODEL], U8, align_bytes=64)
         nc.vector.memset(w_scales[:].bitcast(I32), 0)
+        vector_rows = const.tile([P, P], BF16)
+        nc.vector.memset(vector_rows[:], 0.0)
+        nc.scalar.dma_start(out=vector_rows[0:VECTOR_ROWS, :], in_=ln_a.rearrange("(r c) -> r c", c=P))
+        nc.scalar.dma_start(
+            out=vector_rows[VECTOR_ROWS : 2 * VECTOR_ROWS, :], in_=ln_b.rearrange("(r c) -> r c", c=P)
+        )
 
         features = {}
+        residual = const.tile([P, SENTENCES, D_MODEL], BF16)
 
         def load_features(b, half):
             x = feature_pool.tile([P, HEADS, HALF], BF16)
@@ -70,30 +79,41 @@ def tile_multiheadattention_pa_s_kernel(
             )
             features[(b, half)] = x
 
+        def load_residual(b):
+            nc.sync.dma_start(out=residual[:, b, :], in_=inp[b * P : (b + 1) * P, :])
+
         load_features(0, 0)
         load_scale_rows(nc, w_scales[:, :D_CONTENT], w_proj1_scales[0])
         nc.sync.dma_start(out=w_words[:, : 2 * D_CONTENT].bitcast(I32), in_=w_proj1_words[0].bitcast(I32))
         load_features(0, 1)
         nc.sync.dma_start(out=w_words[:, 2 * D_CONTENT :].bitcast(I32), in_=w_proj2_words[0].bitcast(I32))
         load_scale_rows(nc, w_scales[:, D_CONTENT:], w_proj2_scales[0])
+        load_residual(0)
         for b in range(1, SENTENCES):
-            for half in range(2):
-                load_features(b, half)
-
-        residual = const.tile([P, SENTENCES, D_MODEL], BF16)
-        nc.gpsimd.dma_start(out=residual[:], in_=inp.rearrange("(b l) c -> l b c", l=P))
+            load_features(b, 0)
+            load_features(b, 1)
+            load_residual(b)
 
         identity = const.tile([P, P], F32)
         make_identity(nc, identity[:])
 
-        gain = const.tile([P, D_MODEL], BF16)
-        bias = const.tile([P, D_MODEL], BF16)
-        nc.gpsimd.dma_start(out=gain[:], in_=ln_a.partition_broadcast(P))
-        nc.gpsimd.dma_start(out=bias[:], in_=ln_b.partition_broadcast(P))
-
         one = const.tile([P, 1], F32)
         nc.vector.memset(one[:], 1.0)
         nc.scalar.activation(out=one[:], in_=one[:], func=ACT.Sqrt)
+
+        vector_rows_f32 = const.tile([P, P], F32)
+        nc.vector.tensor_copy(out=vector_rows_f32[:], in_=vector_rows[:])
+        transposed = transposed_pool.tile([P, 2, P], F32)
+        nc.tensor.transpose(transposed[:, 0, :], vector_rows_f32[:], identity[:])
+        vector_columns = const.tile([P, 2 * VECTOR_ROWS], F32)
+        nc.vector.tensor_copy(out=vector_columns[:], in_=transposed[:, 0, : 2 * VECTOR_ROWS])
+        gain = spread_pool.tile([P, D_MODEL], F32)
+        bias = spread_pool.tile([P, D_MODEL], F32)
+
+        def spread(vector, first_column):
+            for r in range(VECTOR_ROWS):
+                column = vector_columns[:, first_column + r : first_column + r + 1]
+                nc.tensor.transpose(vector[:, r * P : (r + 1) * P], column.to_broadcast([P, P]), identity[:])
 
         def project(b):
             z_psum = product_pool.tile([P, D_MODEL], F32)
@@ -124,7 +144,7 @@ def tile_multiheadattention_pa_s_kernel(
                     )
             return z_psum
 
-        def normalise(b, z_psum):
+        def add_residual(b, z_psum):
             z = row_pool.tile([P, D_MODEL], F32)
             row_sum = stat_pool.tile([P, 1], F32)
             nc.vector.scalar_tensor_tensor(
@@ -147,10 +167,16 @@ def tile_multiheadattention_pa_s_kernel(
             )
             sigma = stat_pool.tile([P, 1], F32)
             nc.scalar.activation(out=sigma[:], in_=sum_squares[:], func=ACT.Sqrt, scale=1.0 / (D_MODEL - 1))
+            return z, neg_mean, sigma
+
+        def centre_and_gain(z, neg_mean):
             centred = row_pool.tile([P, D_MODEL], F32)
             nc.vector.scalar_tensor_tensor(
                 out=centred[:], in0=z[:], scalar=neg_mean[:], in1=gain[:], op0=ALU.add, op1=ALU.mult
             )
+            return centred
+
+        def finish(b, centred, sigma):
             inverse = stat_pool.tile([P, 1], F32)
             nc.vector.tensor_scalar(out=inverse[:], in0=sigma[:], scalar1=EPS, scalar2=None, op0=ALU.add)
             nc.vector.reciprocal(out=inverse[:], in_=inverse[:])
@@ -160,8 +186,15 @@ def tile_multiheadattention_pa_s_kernel(
             )
             nc.sync.dma_start(out=out[b * P : (b + 1) * P, :], in_=result[:])
 
-        products = [project(0)]
+        summed = {0: add_residual(0, project(0))}
+        spread(gain, 0)
+        spread(bias, VECTOR_ROWS)
+        product = project(1)
         for b in range(SENTENCES):
+            z, neg_mean, sigma = summed[b]
+            centred = centre_and_gain(z, neg_mean)
             if b + 1 < SENTENCES:
-                products.append(project(b + 1))
-            normalise(b, products[b])
+                summed[b + 1] = add_residual(b + 1, product)
+            finish(b, centred, sigma)
+            if b + 2 < SENTENCES:
+                product = project(b + 2)

@@ -83,9 +83,9 @@ def tile_multiheadattention_pa_s_kernel(
             nc.sync.dma_start(out=residual[:, b, :], in_=inp[b * P : (b + 1) * P, :])
 
         load_features(0, 0)
+        load_features(0, 1)
         load_scale_rows(nc, w_scales[:, :D_CONTENT], w_proj1_scales[0])
         nc.sync.dma_start(out=w_words[:, : 2 * D_CONTENT].bitcast(I32), in_=w_proj1_words[0].bitcast(I32))
-        load_features(0, 1)
         nc.sync.dma_start(out=w_words[:, 2 * D_CONTENT :].bitcast(I32), in_=w_proj2_words[0].bitcast(I32))
         load_scale_rows(nc, w_scales[:, D_CONTENT:], w_proj2_scales[0])
         load_residual(0)

@@ -60,9 +60,9 @@ def tile_multiheadattention_pa_s_kernel(
 
         w_words = const.tile([P, 2 * D_MODEL], U8, align_bytes=64)
         w_scales = const.tile([P, D_MODEL], U8, align_bytes=64)
-        nc.vector.memset(w_scales[:].bitcast(I32), 0)
+        nc.gpsimd.memset(w_scales[:].bitcast(F32), 0.0)
         vector_rows = const.tile([P, P], BF16)
-        nc.vector.memset(vector_rows[:], 0.0)
+        nc.gpsimd.memset(vector_rows[:], 0.0)
         nc.scalar.dma_start(out=vector_rows[0:VECTOR_ROWS, :], in_=ln_a.rearrange("(r c) -> r c", c=P))
         nc.scalar.dma_start(
             out=vector_rows[VECTOR_ROWS : 2 * VECTOR_ROWS, :], in_=ln_b.rearrange("(r c) -> r c", c=P)
@@ -103,10 +103,13 @@ def tile_multiheadattention_pa_s_kernel(
 
         vector_rows_f32 = const.tile([P, P], F32)
         nc.vector.tensor_copy(out=vector_rows_f32[:], in_=vector_rows[:])
-        transposed = transposed_pool.tile([P, 2, P], F32)
-        nc.tensor.transpose(transposed[:, 0, :], vector_rows_f32[:], identity[:])
         vector_columns = const.tile([P, 2 * VECTOR_ROWS], F32)
-        nc.vector.tensor_copy(out=vector_columns[:], in_=transposed[:, 0, : 2 * VECTOR_ROWS])
+
+        def turn_vector_rows():
+            transposed = transposed_pool.tile([P, 2, P], F32)
+            nc.tensor.transpose(transposed[:, 0, :], vector_rows_f32[:], identity[:])
+            nc.vector.tensor_copy(out=vector_columns[:], in_=transposed[:, 0, : 2 * VECTOR_ROWS])
+
         gain = spread_pool.tile([P, D_MODEL], F32)
         bias = spread_pool.tile([P, D_MODEL], F32)
 
@@ -115,8 +118,9 @@ def tile_multiheadattention_pa_s_kernel(
                 column = vector_columns[:, first_column + r : first_column + r + 1]
                 nc.tensor.transpose(vector[:, r * P : (r + 1) * P], column.to_broadcast([P, P]), identity[:])
 
-        def project(b):
-            z_psum = product_pool.tile([P, D_MODEL], F32)
+        operands = {}
+
+        def prepare(b):
             for half in range(2):
                 x_words = features[(b, half)][:].rearrange("l h j -> l (h j)").bitcast(F32)
                 transposed = transposed_pool.tile([P, 2, P], F32)
@@ -131,6 +135,12 @@ def tile_multiheadattention_pa_s_kernel(
                     scales=scales[:],
                     in_=grouped[:].rearrange("p l t -> p (l t)"),
                 )
+                operands[(b, half)] = (codes, scales)
+
+        def multiply(b):
+            z_psum = product_pool.tile([P, D_MODEL], F32)
+            for half in range(2):
+                codes, scales = operands[(b, half)]
                 first, last = (0, D_CONTENT) if half == 0 else (D_CONTENT, D_MODEL)
                 for n in range(first, last, N_GROUP):
                     nc.tensor.matmul_mx(
@@ -157,9 +167,7 @@ def tile_multiheadattention_pa_s_kernel(
                 accum_out=row_sum[:],
             )
             neg_mean = stat_pool.tile([P, 1], F32)
-            nc.vector.tensor_scalar(
-                out=neg_mean[:], in0=row_sum[:], scalar1=-1.0 / D_MODEL, scalar2=None, op0=ALU.mult
-            )
+            nc.scalar.activation(out=neg_mean[:], in_=row_sum[:], func=ACT.Copy, scale=-1.0 / D_MODEL)
             squares = row_pool.tile([P, D_MODEL], BF16)
             sum_squares = stat_pool.tile([P, 1], F32)
             nc.scalar.activation(
@@ -167,6 +175,7 @@ def tile_multiheadattention_pa_s_kernel(
             )
             sigma = stat_pool.tile([P, 1], F32)
             nc.scalar.activation(out=sigma[:], in_=sum_squares[:], func=ACT.Sqrt, scale=1.0 / (D_MODEL - 1))
+            nc.scalar.activation(out=sigma[:], in_=sigma[:], func=ACT.Copy, bias=EPS)
             return z, neg_mean, sigma
 
         def centre_and_gain(z, neg_mean):
@@ -178,15 +187,20 @@ def tile_multiheadattention_pa_s_kernel(
 
         def finish(b, centred, sigma):
             inverse = stat_pool.tile([P, 1], F32)
-            nc.vector.tensor_scalar(out=inverse[:], in0=sigma[:], scalar1=EPS, scalar2=None, op0=ALU.add)
-            nc.vector.reciprocal(out=inverse[:], in_=inverse[:])
+            nc.vector.reciprocal(out=inverse[:], in_=sigma[:])
             result = row_pool.tile([P, D_MODEL], F32)
             nc.vector.scalar_tensor_tensor(
                 out=result[:], in0=centred[:], scalar=inverse[:], in1=bias[:], op0=ALU.mult, op1=ALU.add
             )
             nc.sync.dma_start(out=out[b * P : (b + 1) * P, :], in_=result[:])
 
-        summed = {0: add_residual(0, project(0))}
+        def project(b):
+            prepare(b)
+            return multiply(b)
+
+        prepare(0)
+        turn_vector_rows()
+        summed = {0: add_residual(0, multiply(0))}
         spread(gain, 0)
         spread(bias, VECTOR_ROWS)
         product = project(1)

@@ -51,12 +51,13 @@ def tile_multiheadattention_pa_s_kernel(
     with ExitStack() as ctx:
         const = ctx.enter_context(tc.tile_pool(name="const", bufs=1))
         feature_pool = ctx.enter_context(tc.tile_pool(name="features", bufs=2 * SENTENCES))
-        operand_pool = ctx.enter_context(tc.tile_pool(name="operands", bufs=4))
-        row_pool = ctx.enter_context(tc.tile_pool(name="rows", bufs=3))
-        stat_pool = ctx.enter_context(tc.tile_pool(name="stats", bufs=4))
+        operand_pool = ctx.enter_context(tc.tile_pool(name="operands", bufs=2 * SENTENCES))
+        row_pool = ctx.enter_context(tc.tile_pool(name="rows", bufs=SENTENCES))
+        stat_pool = ctx.enter_context(tc.tile_pool(name="stats", bufs=2 * SENTENCES))
         transposed_pool = ctx.enter_context(tc.psum_pool(name="transposed", bufs=3))
         product_pool = ctx.enter_context(tc.psum_pool(name="product", bufs=3))
         spread_pool = ctx.enter_context(tc.psum_pool(name="spread", bufs=1))
+        ctx.enter_context(tc.manual_schedule())
 
         w_words = const.tile([P, 2 * D_MODEL], U8, align_bytes=64)
         w_scales = const.tile([P, D_MODEL], U8, align_bytes=64)
@@ -118,97 +119,139 @@ def tile_multiheadattention_pa_s_kernel(
                 column = vector_columns[:, first_column + r : first_column + r + 1]
                 nc.tensor.transpose(vector[:, r * P : (r + 1) * P], column.to_broadcast([P, P]), identity[:])
 
+        transposed_words = {}
+        grouped_values = {}
         operands = {}
+        products = {}
+        rows = {}
+        means = {}
+        sums = {}
+        sigmas = {}
+        centred_rows = {}
 
-        def prepare(b):
-            for half in range(2):
-                x_words = features[(b, half)][:].rearrange("l h j -> l (h j)").bitcast(F32)
-                transposed = transposed_pool.tile([P, 2, P], F32)
-                for u in range(2):
-                    nc.tensor.transpose(transposed[:, u, :], x_words[:, u : K // 2 : 2], identity[:])
-                grouped = operand_pool.tile([P, P, 4], BF16, align_bytes=64)
-                nc.scalar.copy(out=grouped[:].bitcast(F32), in_=transposed[:].rearrange("p u l -> p l u"))
-                codes = operand_pool.tile([P, P], U32, align_bytes=64)
-                scales = operand_pool.tile([P, P], U8, align_bytes=64)
-                nc.vector.quantize_mx(
-                    out=codes[:].bitcast(FP8X4),
-                    scales=scales[:],
-                    in_=grouped[:].rearrange("p l t -> p (l t)"),
-                )
-                operands[(b, half)] = (codes, scales)
+        def turn(b, half):
+            x_words = features[(b, half)][:].rearrange("l h j -> l (h j)").bitcast(F32)
+            transposed = transposed_pool.tile([P, 2, P], F32)
+            for u in range(2):
+                nc.tensor.transpose(transposed[:, u, :], x_words[:, u : K // 2 : 2], identity[:])
+            transposed_words[(b, half)] = transposed
+
+        def group(b, half):
+            grouped = operand_pool.tile([P, P, 4], BF16, align_bytes=64)
+            nc.scalar.copy(
+                out=grouped[:].bitcast(F32), in_=transposed_words[(b, half)][:].rearrange("p u l -> p l u")
+            )
+            grouped_values[(b, half)] = grouped
+
+        def quantize(b, half):
+            codes = operand_pool.tile([P, P], U32, align_bytes=64)
+            scales = operand_pool.tile([P, P], U8, align_bytes=64)
+            nc.vector.quantize_mx(
+                out=codes[:].bitcast(FP8X4),
+                scales=scales[:],
+                in_=grouped_values[(b, half)][:].rearrange("p l t -> p (l t)"),
+            )
+            operands[(b, half)] = (codes, scales)
 
         def multiply(b):
             z_psum = product_pool.tile([P, D_MODEL], F32)
-            for half in range(2):
-                codes, scales = operands[(b, half)]
-                first, last = (0, D_CONTENT) if half == 0 else (D_CONTENT, D_MODEL)
-                for n in range(first, last, N_GROUP):
-                    nc.tensor.matmul_mx(
-                        out=z_psum[:, n : n + N_GROUP],
-                        lhsT=codes[:].bitcast(FP8X4),
-                        lhsT_scale=scales[:],
-                        rhs=w_words[:, 2 * n : 2 * (n + N_GROUP)].bitcast(FP4X4),
-                        rhs_scale=w_scales[:, n : n + N_GROUP],
-                        start=True,
-                        stop=True,
-                    )
-            return z_psum
+            for n in range(0, D_MODEL, N_GROUP):
+                codes, scales = operands[(b, 0 if n < D_CONTENT else 1)]
+                nc.tensor.matmul_mx(
+                    out=z_psum[:, n : n + N_GROUP],
+                    lhsT=codes[:].bitcast(FP8X4),
+                    lhsT_scale=scales[:],
+                    rhs=w_words[:, 2 * n : 2 * (n + N_GROUP)].bitcast(FP4X4),
+                    rhs_scale=w_scales[:, n : n + N_GROUP],
+                    start=True,
+                    stop=True,
+                )
+            products[b] = z_psum
 
-        def add_residual(b, z_psum):
+        def add_residual(b):
             z = row_pool.tile([P, D_MODEL], F32)
             row_sum = stat_pool.tile([P, 1], F32)
             nc.vector.scalar_tensor_tensor(
                 out=z[:],
-                in0=z_psum[:],
+                in0=products[b][:],
                 scalar=1.0,
                 in1=residual[:, b, :],
                 op0=ALU.mult,
                 op1=ALU.add,
                 accum_out=row_sum[:],
             )
+            rows[b] = z
+            sums[b] = row_sum
+
+        def square(b):
             neg_mean = stat_pool.tile([P, 1], F32)
-            nc.scalar.activation(out=neg_mean[:], in_=row_sum[:], func=ACT.Copy, scale=-1.0 / D_MODEL)
+            nc.scalar.activation(out=neg_mean[:], in_=sums[b][:], func=ACT.Copy, scale=-1.0 / D_MODEL)
             squares = row_pool.tile([P, D_MODEL], BF16)
             sum_squares = stat_pool.tile([P, 1], F32)
             nc.scalar.activation(
-                out=squares[:], in_=z[:], func=ACT.Square, bias=neg_mean[:], accum_out=sum_squares[:]
+                out=squares[:], in_=rows[b][:], func=ACT.Square, bias=neg_mean[:], accum_out=sum_squares[:]
             )
-            sigma = stat_pool.tile([P, 1], F32)
-            nc.scalar.activation(out=sigma[:], in_=sum_squares[:], func=ACT.Sqrt, scale=1.0 / (D_MODEL - 1))
-            nc.scalar.activation(out=sigma[:], in_=sigma[:], func=ACT.Copy, bias=EPS)
-            return z, neg_mean, sigma
+            means[b] = neg_mean
+            sums[b] = sum_squares
 
-        def centre_and_gain(z, neg_mean):
+        def root(b):
+            sigma = stat_pool.tile([P, 1], F32)
+            nc.scalar.activation(out=sigma[:], in_=sums[b][:], func=ACT.Sqrt, scale=1.0 / (D_MODEL - 1))
+            nc.scalar.activation(out=sigma[:], in_=sigma[:], func=ACT.Copy, bias=EPS)
+            sigmas[b] = sigma
+
+        def centre_and_gain(b):
             centred = row_pool.tile([P, D_MODEL], F32)
             nc.vector.scalar_tensor_tensor(
-                out=centred[:], in0=z[:], scalar=neg_mean[:], in1=gain[:], op0=ALU.add, op1=ALU.mult
+                out=centred[:], in0=rows[b][:], scalar=means[b][:], in1=gain[:], op0=ALU.add, op1=ALU.mult
             )
-            return centred
+            centred_rows[b] = centred
 
-        def finish(b, centred, sigma):
+        def finish(b):
             inverse = stat_pool.tile([P, 1], F32)
-            nc.vector.reciprocal(out=inverse[:], in_=sigma[:])
+            nc.vector.reciprocal(out=inverse[:], in_=sigmas[b][:])
             result = row_pool.tile([P, D_MODEL], F32)
             nc.vector.scalar_tensor_tensor(
-                out=result[:], in0=centred[:], scalar=inverse[:], in1=bias[:], op0=ALU.mult, op1=ALU.add
+                out=result[:], in0=centred_rows[b][:], scalar=inverse[:], in1=bias[:], op0=ALU.mult, op1=ALU.add
             )
             nc.sync.dma_start(out=out[b * P : (b + 1) * P, :], in_=result[:])
 
-        def project(b):
-            prepare(b)
-            return multiply(b)
-
-        prepare(0)
         turn_vector_rows()
-        summed = {0: add_residual(0, multiply(0))}
+        turn(0, 0)
+        group(0, 0)
+        turn(0, 1)
+        group(0, 1)
+        quantize(0, 0)
+        quantize(0, 1)
         spread(gain, 0)
         spread(bias, VECTOR_ROWS)
-        product = project(1)
-        for b in range(SENTENCES):
-            z, neg_mean, sigma = summed[b]
-            centred = centre_and_gain(z, neg_mean)
-            if b + 1 < SENTENCES:
-                summed[b + 1] = add_residual(b + 1, product)
-            finish(b, centred, sigma)
-            if b + 2 < SENTENCES:
-                product = project(b + 2)
+        multiply(0)
+        add_residual(0)
+        turn(1, 0)
+        group(1, 0)
+        square(0)
+        quantize(1, 0)
+        centre_and_gain(0)
+        turn(1, 1)
+        group(1, 1)
+        root(0)
+        quantize(1, 1)
+        finish(0)
+        for b in (2, 3):
+            for half in range(2):
+                turn(b, half)
+                group(b, half)
+            multiply(b - 1)
+            for half in range(2):
+                quantize(b, half)
+            add_residual(b - 1)
+        multiply(3)
+        for b in (1, 2):
+            square(b)
+            root(b)
+        add_residual(3)
+        square(3)
+        root(3)
+        for b in (1, 2, 3):
+            centre_and_gain(b)
+            finish(b)

@@ -216,13 +216,13 @@ def tile_multiheadattention_pa_s_kernel(
             )
             nc.sync.dma_start(out=out[b * P : (b + 1) * P, :], in_=result[:])
 
-        turn_vector_rows()
         turn(0, 0)
         group(0, 0)
         turn(0, 1)
         group(0, 1)
         quantize(0, 0)
         quantize(0, 1)
+        turn_vector_rows()
         spread(gain, 0)
         spread(bias, VECTOR_ROWS)
         multiply(0)

@@ -207,14 +207,26 @@ def tile_multiheadattention_pa_s_kernel(
             )
             centred_rows[b] = centred
 
-        def finish(b):
+        inverses = {}
+
+        def invert(b):
             inverse = stat_pool.tile([P, 1], F32)
             nc.vector.reciprocal(out=inverse[:], in_=sigmas[b][:])
+            inverses[b] = inverse
+
+        def finish(b, pieces):
             result = row_pool.tile([P, D_MODEL], F32)
-            nc.vector.scalar_tensor_tensor(
-                out=result[:], in0=centred_rows[b][:], scalar=inverse[:], in1=bias[:], op0=ALU.mult, op1=ALU.add
-            )
-            nc.sync.dma_start(out=out[b * P : (b + 1) * P, :], in_=result[:])
+            width = D_MODEL // pieces
+            for n in range(0, D_MODEL, width):
+                nc.vector.scalar_tensor_tensor(
+                    out=result[:, n : n + width],
+                    in0=centred_rows[b][:, n : n + width],
+                    scalar=inverses[b][:],
+                    in1=bias[:, n : n + width],
+                    op0=ALU.mult,
+                    op1=ALU.add,
+                )
+                nc.sync.dma_start(out=out[b * P : (b + 1) * P, n : n + width], in_=result[:, n : n + width])
 
         turn(0, 0)
         group(0, 0)
@@ -236,7 +248,8 @@ def tile_multiheadattention_pa_s_kernel(
         group(1, 1)
         root(0)
         quantize(1, 1)
-        finish(0)
+        invert(0)
+        finish(0, 1)
         for b in (2, 3):
             for half in range(2):
                 turn(b, half)
@@ -252,6 +265,12 @@ def tile_multiheadattention_pa_s_kernel(
         add_residual(3)
         square(3)
         root(3)
-        for b in (1, 2, 3):
-            centre_and_gain(b)
-            finish(b)
+        centre_and_gain(1)
+        invert(1)
+        centre_and_gain(2)
+        finish(1, 1)
+        invert(2)
+        centre_and_gain(3)
+        finish(2, 1)
+        invert(3)
+        finish(3, 2)

@@ -185,7 +185,9 @@ def tile_multiheadattention_pa_s_kernel(
 
         def square(b):
             neg_mean = stat_pool.tile([P, 1], F32)
-            nc.scalar.activation(out=neg_mean[:], in_=sums[b][:], func=ACT.Copy, scale=-1.0 / D_MODEL)
+            nc.gpsimd.tensor_scalar(
+                out=neg_mean[:], in0=sums[b][:], scalar1=-1.0 / D_MODEL, scalar2=0.0, op0=ALU.mult, op1=ALU.add
+            )
             squares = row_pool.tile([P, D_MODEL], BF16)
             sum_squares = stat_pool.tile([P, 1], F32)
             nc.scalar.activation(

@@ -191,14 +191,19 @@ def tile_multiheadattention_pa_s_kernel(
             squares = row_pool.tile([P, D_MODEL], BF16)
             sum_squares = stat_pool.tile([P, 1], F32)
             nc.scalar.activation(
-                out=squares[:], in_=rows[b][:], func=ACT.Square, bias=neg_mean[:], accum_out=sum_squares[:]
+                out=squares[:],
+                in_=rows[b][:],
+                func=ACT.Square,
+                bias=sums[b][:],
+                scale=-float(D_MODEL),
+                accum_out=sum_squares[:],
             )
             means[b] = neg_mean
             sums[b] = sum_squares
 
         def root(b):
             sigma = stat_pool.tile([P, 1], F32)
-            nc.scalar.activation(out=sigma[:], in_=sums[b][:], func=ACT.Sqrt, scale=1.0 / (D_MODEL - 1))
+            nc.scalar.activation(out=sigma[:], in_=sums[b][:], func=ACT.Sqrt, scale=1.0 / (D_MODEL * D_MODEL * (D_MODEL - 1)))
             nc.scalar.activation(out=sigma[:], in_=sigma[:], func=ACT.Copy, bias=EPS)
             sigmas[b] = sigma
 

@@ -23,6 +23,7 @@ D_MODEL = 512
 N_GROUP = 128
 VECTOR_ROWS = D_MODEL // P
 EPS = 1e-3
+ROOT_SCALE = 1.0 / (D_MODEL * D_MODEL * (D_MODEL - 1))
 
 FLOPS = 2 * SENTENCES * P * K * D_MODEL
 
@@ -98,9 +99,13 @@ def tile_multiheadattention_pa_s_kernel(
         identity = const.tile([P, P], F32)
         make_identity(nc, identity[:])
 
-        one = const.tile([P, 1], F32)
+        one = const.tile([P, SENTENCES], F32)
         nc.vector.memset(one[:], 1.0)
-        nc.scalar.activation(out=one[:], in_=one[:], func=ACT.Sqrt)
+        nc.scalar.activation(out=one[:, 0:1], in_=one[:, 0:1], func=ACT.Sqrt)
+        under_root = const.tile([P, 2, SENTENCES], F32)
+        nc.vector.tensor_scalar(
+            out=under_root[:, 1, :], in0=one[:], scalar1=EPS * EPS / ROOT_SCALE, scalar2=None, op0=ALU.mult
+        )
 
         vector_rows_f32 = const.tile([P, P], F32)
         nc.vector.tensor_copy(out=vector_rows_f32[:], in_=vector_rows[:])
@@ -189,23 +194,23 @@ def tile_multiheadattention_pa_s_kernel(
                 out=neg_mean[:], in0=sums[b][:], scalar1=-1.0 / D_MODEL, scalar2=0.0, op0=ALU.mult, op1=ALU.add
             )
             squares = row_pool.tile([P, D_MODEL], BF16)
-            sum_squares = stat_pool.tile([P, 1], F32)
             nc.scalar.activation(
                 out=squares[:],
                 in_=rows[b][:],
                 func=ACT.Square,
                 bias=sums[b][:],
                 scale=-float(D_MODEL),
-                accum_out=sum_squares[:],
+                accum_out=under_root[:, 0, b : b + 1],
             )
             means[b] = neg_mean
-            sums[b] = sum_squares
 
         def root(b):
-            sigma = stat_pool.tile([P, 1], F32)
-            nc.scalar.activation(out=sigma[:], in_=sums[b][:], func=ACT.Sqrt, scale=1.0 / (D_MODEL * D_MODEL * (D_MODEL - 1)))
-            nc.scalar.activation(out=sigma[:], in_=sigma[:], func=ACT.Copy, bias=EPS)
-            sigmas[b] = sigma
+            roots = stat_pool.tile([P, 2], F32)
+            sigma_eps = stat_pool.tile([P, 1], F32)
+            nc.scalar.activation(
+                out=roots[:], in_=under_root[:, :, b], func=ACT.Sqrt, scale=ROOT_SCALE, accum_out=sigma_eps[:]
+            )
+            sigmas[b] = sigma_eps
 
         def centre_and_gain(b):
             centred = row_pool.tile([P, D_MODEL], F32)

@@ -17,6 +17,7 @@ P = 128
 HEADS = 8
 HALF = 64
 SENTENCES = 4
+STRIPES = SENTENCES
 K = HEADS * HALF
 D_CONTENT = 384
 D_MODEL = 512
@@ -28,8 +29,8 @@ ROOT_SCALE = 1.0 / (D_MODEL * D_MODEL * (D_MODEL - 1))
 FLOPS = 2 * SENTENCES * P * K * D_MODEL
 
 
-def load_scale_rows(nc, plane, scale_rows):
-    for a in range(4):
+def load_scale_rows(nc, plane, scale_rows, quarters):
+    for a in quarters:
         nc.sync.dma_start(
             out=plane[32 * a : 32 * a + 4, :].bitcast(I32),
             in_=scale_rows[4 * a : 4 * a + 4, :].bitcast(I32),
@@ -64,48 +65,53 @@ def tile_multiheadattention_pa_s_kernel(
         w_scales = const.tile([P, D_MODEL], U8, align_bytes=64)
         nc.gpsimd.memset(w_scales[:].bitcast(F32), 0.0)
         vector_rows = const.tile([P, P], BF16)
-        nc.gpsimd.memset(vector_rows[:], 0.0)
+        nc.vector.memset(vector_rows[:], 0.0)
         nc.scalar.dma_start(out=vector_rows[0:VECTOR_ROWS, :], in_=ln_a.rearrange("(r c) -> r c", c=P))
         nc.scalar.dma_start(
             out=vector_rows[VECTOR_ROWS : 2 * VECTOR_ROWS, :], in_=ln_b.rearrange("(r c) -> r c", c=P)
         )
 
         features = {}
+        raw_features = {}
         residual = const.tile([P, SENTENCES, D_MODEL], BF16)
 
-        def load_features(b, half):
+        attn_stripes = attn_out.rearrange("h b l f -> h (b l) f").rearrange("h (p s) f -> p h s f", s=STRIPES)
+        inp_stripes = inp.rearrange("(p s) d -> p s d", s=STRIPES)
+        out_stripes = out.rearrange("(p s) d -> p s d", s=STRIPES)
+
+        def load_half(s, half):
             x = feature_pool.tile([P, HEADS, HALF], BF16)
-            nc.sync.dma_start(
-                out=x[:],
-                in_=attn_out[:, b, :, half * HALF : (half + 1) * HALF].rearrange("h l j -> l h j"),
-            )
-            features[(b, half)] = x
+            nc.sync.dma_start(out=x[:], in_=attn_stripes[:, :, s, half * HALF : (half + 1) * HALF])
+            features[(s, half)] = x
 
-        def load_residual(b):
-            nc.sync.dma_start(out=residual[:, b, :], in_=inp[b * P : (b + 1) * P, :])
+        def load_whole(first, last):
+            raw = const.tile([P, HEADS, last - first, 2 * HALF], BF16, name=f"raw_{first}")
+            nc.sync.dma_start(out=raw[:], in_=attn_stripes[:, :, first:last, :])
+            for s in range(first, last):
+                raw_features[s] = raw[:, :, s - first, :]
 
-        load_features(0, 0)
-        load_features(0, 1)
-        load_scale_rows(nc, w_scales[:, :D_CONTENT], w_proj1_scales[0])
+        def load_residual(first, last):
+            nc.gpsimd.dma_start(out=residual[:, first:last, :], in_=inp_stripes[:, first:last, :])
+
+        load_half(0, 0)
+        load_half(0, 1)
+        load_scale_rows(nc, w_scales[:, :D_CONTENT], w_proj1_scales[0], range(3))
+        load_whole(1, 2)
+        load_scale_rows(nc, w_scales[:, :D_CONTENT], w_proj1_scales[0], range(3, 4))
         nc.sync.dma_start(out=w_words[:, : 2 * D_CONTENT].bitcast(I32), in_=w_proj1_words[0].bitcast(I32))
         nc.sync.dma_start(out=w_words[:, 2 * D_CONTENT :].bitcast(I32), in_=w_proj2_words[0].bitcast(I32))
-        load_scale_rows(nc, w_scales[:, D_CONTENT:], w_proj2_scales[0])
-        load_residual(0)
-        for b in range(1, SENTENCES):
-            load_features(b, 0)
-            load_features(b, 1)
-            load_residual(b)
+        load_scale_rows(nc, w_scales[:, D_CONTENT:], w_proj2_scales[0], range(4))
+        load_whole(2, 4)
 
         identity = const.tile([P, P], F32)
         make_identity(nc, identity[:])
+        load_residual(0, 2)
+        load_residual(2, 4)
 
-        one = const.tile([P, SENTENCES], F32)
+        one = const.tile([P, 1], F32)
         nc.vector.memset(one[:], 1.0)
-        nc.scalar.activation(out=one[:, 0:1], in_=one[:, 0:1], func=ACT.Sqrt)
-        under_root = const.tile([P, 2, SENTENCES], F32)
-        nc.vector.tensor_scalar(
-            out=under_root[:, 1, :], in0=one[:], scalar1=EPS * EPS / ROOT_SCALE, scalar2=None, op0=ALU.mult
-        )
+        root_of_one = const.tile([P, 1], F32)
+        nc.scalar.activation(out=root_of_one[:], in_=one[:], func=ACT.Sqrt)
 
         vector_rows_f32 = const.tile([P, P], F32)
         nc.vector.tensor_copy(out=vector_rows_f32[:], in_=vector_rows[:])
@@ -124,6 +130,7 @@ def tile_multiheadattention_pa_s_kernel(
                 column = vector_columns[:, first_column + r : first_column + r + 1]
                 nc.tensor.transpose(vector[:, r * P : (r + 1) * P], column.to_broadcast([P, P]), identity[:])
 
+        sorted_words = {}
         transposed_words = {}
         grouped_values = {}
         operands = {}
@@ -131,15 +138,25 @@ def tile_multiheadattention_pa_s_kernel(
         rows = {}
         means = {}
         sums = {}
+        square_sums = {}
         sigmas = {}
         centred_rows = {}
 
-        def turn(b, half):
-            x_words = features[(b, half)][:].rearrange("l h j -> l (h j)").bitcast(F32)
+        def sort(s, half):
+            words = raw_features[s][:, :, half * HALF : (half + 1) * HALF].bitcast(F32)
+            x = feature_pool.tile([P, 2, HEADS, HALF // 4], F32, name="sorted_words")
+            nc.vector.tensor_copy(out=x[:], in_=words.rearrange("l h (i u) -> l u h i", u=2))
+            sorted_words[(s, half)] = x
+
+        def turn(s, half):
             transposed = transposed_pool.tile([P, 2, P], F32)
             for u in range(2):
-                nc.tensor.transpose(transposed[:, u, :], x_words[:, u : K // 2 : 2], identity[:])
-            transposed_words[(b, half)] = transposed
+                if s == 0:
+                    words = features[(s, half)][:].rearrange("l h j -> l (h j)").bitcast(F32)[:, u : K // 2 : 2]
+                else:
+                    words = sorted_words[(s, half)][:, u, :, :].rearrange("l h i -> l (h i)")
+                nc.tensor.transpose(transposed[:, u, :], words, identity[:])
+            transposed_words[(s, half)] = transposed
 
         def group(b, half):
             grouped = operand_pool.tile([P, P, 4], BF16, align_bytes=64)
@@ -187,30 +204,30 @@ def tile_multiheadattention_pa_s_kernel(
             )
             rows[b] = z
             sums[b] = row_sum
-
-        def square(b):
             neg_mean = stat_pool.tile([P, 1], F32)
             nc.gpsimd.tensor_scalar(
-                out=neg_mean[:], in0=sums[b][:], scalar1=-1.0 / D_MODEL, scalar2=0.0, op0=ALU.mult, op1=ALU.add
+                out=neg_mean[:], in0=row_sum[:], scalar1=-1.0 / D_MODEL, scalar2=0.0, op0=ALU.mult, op1=ALU.add
             )
+            means[b] = neg_mean
+
+        def square(b):
             squares = row_pool.tile([P, D_MODEL], BF16)
+            sum_squares = stat_pool.tile([P, 1], F32)
             nc.scalar.activation(
                 out=squares[:],
                 in_=rows[b][:],
                 func=ACT.Square,
                 bias=sums[b][:],
                 scale=-float(D_MODEL),
-                accum_out=under_root[:, 0, b : b + 1],
+                accum_out=sum_squares[:],
             )
-            means[b] = neg_mean
+            square_sums[b] = sum_squares
 
         def root(b):
-            roots = stat_pool.tile([P, 2], F32)
-            sigma_eps = stat_pool.tile([P, 1], F32)
-            nc.scalar.activation(
-                out=roots[:], in_=under_root[:, :, b], func=ACT.Sqrt, scale=ROOT_SCALE, accum_out=sigma_eps[:]
-            )
-            sigmas[b] = sigma_eps
+            sigma = stat_pool.tile([P, 1], F32)
+            nc.scalar.activation(out=sigma[:], in_=square_sums[b][:], func=ACT.Sqrt, scale=ROOT_SCALE)
+            nc.scalar.activation(out=sigma[:], in_=sigma[:], func=ACT.Copy, bias=EPS)
+            sigmas[b] = sigma
 
         def centre_and_gain(b):
             centred = row_pool.tile([P, D_MODEL], F32)
@@ -238,48 +255,63 @@ def tile_multiheadattention_pa_s_kernel(
                     op0=ALU.mult,
                     op1=ALU.add,
                 )
-                nc.sync.dma_start(out=out[b * P : (b + 1) * P, n : n + width], in_=result[:, n : n + width])
+                nc.sync.dma_start(out=out_stripes[:, b, n : n + width], in_=result[:, n : n + width])
 
         turn(0, 0)
         group(0, 0)
         turn(0, 1)
         group(0, 1)
+        turn_vector_rows()
         quantize(0, 0)
         quantize(0, 1)
-        turn_vector_rows()
+        sort(1, 0)
+        sort(1, 1)
         spread(gain, 0)
-        spread(bias, VECTOR_ROWS)
-        multiply(0)
-        add_residual(0)
         turn(1, 0)
         group(1, 0)
-        square(0)
-        quantize(1, 0)
-        centre_and_gain(0)
         turn(1, 1)
         group(1, 1)
-        root(0)
+        multiply(0)
+        add_residual(0)
+        spread(bias, VECTOR_ROWS)
+        quantize(1, 0)
         quantize(1, 1)
-        invert(0)
-        finish(0, 1)
-        for b in (2, 3):
-            for half in range(2):
-                turn(b, half)
-                group(b, half)
-            multiply(b - 1)
-            for half in range(2):
-                quantize(b, half)
-            add_residual(b - 1)
+        sort(2, 0)
+        sort(2, 1)
+        multiply(1)
+        square(0)
+        centre_and_gain(0)
+        sort(3, 0)
+        sort(3, 1)
+        turn(2, 0)
+        group(2, 0)
+        turn(2, 1)
+        group(2, 1)
+        root(0)
+        add_residual(1)
+        turn(3, 0)
+        group(3, 0)
+        turn(3, 1)
+        group(3, 1)
+        quantize(2, 0)
+        quantize(2, 1)
+        square(1)
+        multiply(2)
+        quantize(3, 0)
+        quantize(3, 1)
+        add_residual(2)
         multiply(3)
-        for b in (1, 2):
-            square(b)
-            root(b)
+        invert(0)
+        root(1)
         add_residual(3)
-        square(3)
-        root(3)
+        square(2)
+        finish(0, 1)
+        root(2)
         centre_and_gain(1)
+        square(3)
         invert(1)
         centre_and_gain(2)
+        root(3)
         finish(1, 1)
         invert(2)
         centre_and_gain(3)

@@ -61,10 +61,10 @@ def tile_multiheadattention_pa_s_kernel(
         spread_pool = ctx.enter_context(tc.psum_pool(name="spread", bufs=1))
         ctx.enter_context(tc.manual_schedule())
 
-        w_words = const.tile([P, 2 * D_MODEL], U8, align_bytes=64)
-        w_scales = const.tile([P, D_MODEL], U8, align_bytes=64)
+        w_words = const.tile([P, 2 * D_MODEL], U8, align_bytes=512)
+        w_scales = const.tile([P, D_MODEL], U8, align_bytes=512)
         nc.gpsimd.memset(w_scales[:].bitcast(F32), 0.0)
-        vector_rows = const.tile([P, P], BF16)
+        vector_rows = const.tile([P, P], BF16, align_bytes=512)
         nc.vector.memset(vector_rows[:], 0.0)
         nc.scalar.dma_start(out=vector_rows[0:VECTOR_ROWS, :], in_=ln_a.rearrange("(r c) -> r c", c=P))
         nc.scalar.dma_start(
@@ -73,19 +73,19 @@ def tile_multiheadattention_pa_s_kernel(
 
         features = {}
         raw_features = {}
-        residual = const.tile([P, SENTENCES, D_MODEL], BF16)
+        residual = const.tile([P, SENTENCES, D_MODEL], BF16, align_bytes=512)
 
         attn_stripes = attn_out.rearrange("h b l f -> h (b l) f").rearrange("h (p s) f -> p h s f", s=STRIPES)
         inp_stripes = inp.rearrange("(p s) d -> p s d", s=STRIPES)
         out_stripes = out.rearrange("(p s) d -> p s d", s=STRIPES)
 
         def load_half(s, half):
-            x = feature_pool.tile([P, HEADS, HALF], BF16)
+            x = feature_pool.tile([P, HEADS, HALF], BF16, align_bytes=512)
             nc.sync.dma_start(out=x[:], in_=attn_stripes[:, :, s, half * HALF : (half + 1) * HALF])
             features[(s, half)] = x
 
         def load_whole(first, last):
-            raw = const.tile([P, HEADS, last - first, 2 * HALF], BF16, name=f"raw_{first}")
+            raw = const.tile([P, HEADS, last - first, 2 * HALF], BF16, name=f"raw_{first}", align_bytes=512)
             nc.sync.dma_start(out=raw[:], in_=attn_stripes[:, :, first:last, :])
             for s in range(first, last):
                 raw_features[s] = raw[:, :, s - first, :]
@@ -108,10 +108,14 @@ def tile_multiheadattention_pa_s_kernel(
         load_residual(0, 2)
         load_residual(2, 4)
 
-        one = const.tile([P, 1], F32)
+        one = const.tile([P, SENTENCES], F32)
         nc.vector.memset(one[:], 1.0)
         root_of_one = const.tile([P, 1], F32)
-        nc.scalar.activation(out=root_of_one[:], in_=one[:], func=ACT.Sqrt)
+        nc.scalar.activation(out=root_of_one[:], in_=one[:, 0:1], func=ACT.Sqrt)
+        under_root = const.tile([P, 2, SENTENCES], F32)
+        nc.vector.tensor_scalar(
+            out=under_root[:, 1, :], in0=one[:], scalar1=EPS * EPS / ROOT_SCALE, scalar2=None, op0=ALU.mult
+        )
 
         vector_rows_f32 = const.tile([P, P], F32)
         nc.vector.tensor_copy(out=vector_rows_f32[:], in_=vector_rows[:])
@@ -138,14 +142,14 @@ def tile_multiheadattention_pa_s_kernel(
         rows = {}
         means = {}
         sums = {}
-        square_sums = {}
         sigmas = {}
         centred_rows = {}
 
         def sort(s, half):
             words = raw_features[s][:, :, half * HALF : (half + 1) * HALF].bitcast(F32)
-            x = feature_pool.tile([P, 2, HEADS, HALF // 4], F32, name="sorted_words")
-            nc.vector.tensor_copy(out=x[:], in_=words.rearrange("l h (i u) -> l u h i", u=2))
+            x = feature_pool.tile([P, 2, HEADS, HALF // 4], F32, name="sorted_words", align_bytes=512)
+            copy = nc.vector.tensor_copy if s == 1 else nc.scalar.copy
+            copy(out=x[:], in_=words.rearrange("l h (i u) -> l u h i", u=2))
             sorted_words[(s, half)] = x
 
         def turn(s, half):
@@ -159,15 +163,15 @@ def tile_multiheadattention_pa_s_kernel(
             transposed_words[(s, half)] = transposed
 
         def group(b, half):
-            grouped = operand_pool.tile([P, P, 4], BF16, align_bytes=64)
+            grouped = operand_pool.tile([P, P, 4], BF16, align_bytes=512)
             nc.scalar.copy(
                 out=grouped[:].bitcast(F32), in_=transposed_words[(b, half)][:].rearrange("p u l -> p l u")
             )
             grouped_values[(b, half)] = grouped
 
         def quantize(b, half):
-            codes = operand_pool.tile([P, P], U32, align_bytes=64)
-            scales = operand_pool.tile([P, P], U8, align_bytes=64)
+            codes = operand_pool.tile([P, P], U32, align_bytes=512)
+            scales = operand_pool.tile([P, P], U8, align_bytes=512)
             nc.vector.quantize_mx(
                 out=codes[:].bitcast(FP8X4),
                 scales=scales[:],
@@ -191,7 +195,7 @@ def tile_multiheadattention_pa_s_kernel(
             products[b] = z_psum
 
         def add_residual(b):
-            z = row_pool.tile([P, D_MODEL], F32)
+            z = row_pool.tile([P, D_MODEL], F32, align_bytes=512)
             row_sum = stat_pool.tile([P, 1], F32)
             nc.vector.scalar_tensor_tensor(
                 out=z[:],
@@ -211,26 +215,26 @@ def tile_multiheadattention_pa_s_kernel(
             means[b] = neg_mean
 
         def square(b):
-            squares = row_pool.tile([P, D_MODEL], BF16)
-            sum_squares = stat_pool.tile([P, 1], F32)
+            squares = row_pool.tile([P, D_MODEL], BF16, align_bytes=512)
             nc.scalar.activation(
                 out=squares[:],
                 in_=rows[b][:],
                 func=ACT.Square,
                 bias=sums[b][:],
                 scale=-float(D_MODEL),
-                accum_out=sum_squares[:],
+                accum_out=under_root[:, 0, b : b + 1],
             )
-            square_sums[b] = sum_squares
 
         def root(b):
-            sigma = stat_pool.tile([P, 1], F32)
-            nc.scalar.activation(out=sigma[:], in_=square_sums[b][:], func=ACT.Sqrt, scale=ROOT_SCALE)
-            nc.scalar.activation(out=sigma[:], in_=sigma[:], func=ACT.Copy, bias=EPS)
-            sigmas[b] = sigma
+            roots = stat_pool.tile([P, 2], F32)
+            sigma_eps = stat_pool.tile([P, 1], F32)
+            nc.scalar.activation(
+                out=roots[:], in_=under_root[:, :, b], func=ACT.Sqrt, scale=ROOT_SCALE, accum_out=sigma_eps[:]
+            )
+            sigmas[b] = sigma_eps
 
         def centre_and_gain(b):
-            centred = row_pool.tile([P, D_MODEL], F32)
+            centred = row_pool.tile([P, D_MODEL], F32, align_bytes=512)
             nc.vector.scalar_tensor_tensor(
                 out=centred[:], in0=rows[b][:], scalar=means[b][:], in1=gain[:], op0=ALU.add, op1=ALU.mult
             )
@@ -244,7 +248,7 @@ def tile_multiheadattention_pa_s_kernel(
             inverses[b] = inverse
 
         def finish(b, pieces):
-            result = row_pool.tile([P, D_MODEL], F32)
+            result = row_pool.tile([P, D_MODEL], F32, align_bytes=512)
             width = D_MODEL // pieces
             for n in range(0, D_MODEL, width):
                 nc.vector.scalar_tensor_tensor(
@@ -276,36 +280,36 @@ def tile_multiheadattention_pa_s_kernel(
         spread(bias, VECTOR_ROWS)
         quantize(1, 0)
         quantize(1, 1)
-        sort(2, 0)
-        sort(2, 1)
         multiply(1)
         square(0)
-        centre_and_gain(0)
+        root(0)
+        sort(2, 0)
+        sort(2, 1)
         sort(3, 0)
         sort(3, 1)
+        centre_and_gain(0)
         turn(2, 0)
         group(2, 0)
         turn(2, 1)
         group(2, 1)
-        root(0)
         add_residual(1)
         turn(3, 0)
         group(3, 0)
         turn(3, 1)
         group(3, 1)
+        invert(0)
+        finish(0, 1)
         quantize(2, 0)
         quantize(2, 1)
-        square(1)
         multiply(2)
+        square(1)
         quantize(3, 0)
         quantize(3, 1)
-        add_residual(2)
         multiply(3)
-        invert(0)
         root(1)
-        add_residual(3)
+        add_residual(2)
         square(2)
-        finish(0, 1)
+        add_residual(3)
         root(2)
         centre_and_gain(1)
         square(3)

@@ -101,7 +101,9 @@ def tile_multiheadattention_pa_s_kernel(
         nc.sync.dma_start(out=w_words[:, : 2 * D_CONTENT].bitcast(I32), in_=w_proj1_words[0].bitcast(I32))
         nc.sync.dma_start(out=w_words[:, 2 * D_CONTENT :].bitcast(I32), in_=w_proj2_words[0].bitcast(I32))
         load_scale_rows(nc, w_scales[:, D_CONTENT:], w_proj2_scales[0], range(4))
-        load_whole(2, 4)
+        for s in (2, 3):
+            load_half(s, 0)
+            load_half(s, 1)
 
         identity = const.tile([P, P], F32)
         make_identity(nc, identity[:])
@@ -148,14 +150,13 @@ def tile_multiheadattention_pa_s_kernel(
         def sort(s, half):
             words = raw_features[s][:, :, half * HALF : (half + 1) * HALF].bitcast(F32)
             x = feature_pool.tile([P, 2, HEADS, HALF // 4], F32, name="sorted_words", align_bytes=512)
-            copy = nc.vector.tensor_copy if s == 1 else nc.scalar.copy
-            copy(out=x[:], in_=words.rearrange("l h (i u) -> l u h i", u=2))
+            nc.vector.tensor_copy(out=x[:], in_=words.rearrange("l h (i u) -> l u h i", u=2))
             sorted_words[(s, half)] = x
 
         def turn(s, half):
             transposed = transposed_pool.tile([P, 2, P], F32)
             for u in range(2):
-                if s == 0:
+                if (s, half) in features:
                     words = features[(s, half)][:].rearrange("l h j -> l (h j)").bitcast(F32)[:, u : K // 2 : 2]
                 else:
                     words = sorted_words[(s, half)][:, u, :, :].rearrange("l h i -> l (h i)")
@@ -270,12 +271,12 @@ def tile_multiheadattention_pa_s_kernel(
         quantize(0, 1)
         sort(1, 0)
         sort(1, 1)
-        spread(gain, 0)
         turn(1, 0)
         group(1, 0)
         turn(1, 1)
         group(1, 1)
         multiply(0)
+        spread(gain, 0)
         add_residual(0)
         spread(bias, VECTOR_ROWS)
         quantize(1, 0)
@@ -283,10 +284,6 @@ def tile_multiheadattention_pa_s_kernel(
         multiply(1)
         square(0)
         root(0)
-        sort(2, 0)
-        sort(2, 1)
-        sort(3, 0)
-        sort(3, 1)
         centre_and_gain(0)
         turn(2, 0)
         group(2, 0)

@@ -21,7 +21,7 @@ STRIPES = SENTENCES
 K = HEADS * HALF
 D_CONTENT = 384
 D_MODEL = 512
-N_GROUP = 128
+COLUMN_GROUPS = ((0, 256), (256, 128), (384, 128))
 VECTOR_ROWS = D_MODEL // P
 EPS = 1e-3
 ROOT_SCALE = 1.0 / (D_MODEL * D_MODEL * (D_MODEL - 1))
@@ -182,14 +182,14 @@ def tile_multiheadattention_pa_s_kernel(
 
         def multiply(b):
             z_psum = product_pool.tile([P, D_MODEL], F32)
-            for n in range(0, D_MODEL, N_GROUP):
+            for n, width in COLUMN_GROUPS:
                 codes, scales = operands[(b, 0 if n < D_CONTENT else 1)]
                 nc.tensor.matmul_mx(
-                    out=z_psum[:, n : n + N_GROUP],
+                    out=z_psum[:, n : n + width],
                     lhsT=codes[:].bitcast(FP8X4),
                     lhsT_scale=scales[:],
-                    rhs=w_words[:, 2 * n : 2 * (n + N_GROUP)].bitcast(FP4X4),
-                    rhs_scale=w_scales[:, n : n + N_GROUP],
+                    rhs=w_words[:, 2 * n : 2 * (n + width)].bitcast(FP4X4),
+                    rhs_scale=w_scales[:, n : n + width],
                     start=True,
                     stop=True,
                 )
@@ -271,12 +271,12 @@ def tile_multiheadattention_pa_s_kernel(
         quantize(0, 1)
         sort(1, 0)
         sort(1, 1)
+        spread(gain, 0)
         turn(1, 0)
         group(1, 0)
         turn(1, 1)
         group(1, 1)
         multiply(0)
-        spread(gain, 0)
         add_residual(0)
         spread(bias, VECTOR_ROWS)
         quantize(1, 0)
@@ -295,8 +295,8 @@ def tile_multiheadattention_pa_s_kernel(
         turn(3, 1)
         group(3, 1)
         invert(0)
-        finish(0, 1)
         quantize(2, 0)
+        finish(0, 1)
         quantize(2, 1)
         multiply(2)
         square(1)
@@ -304,18 +304,18 @@ def tile_multiheadattention_pa_s_kernel(
         quantize(3, 1)
         multiply(3)
         root(1)
+        centre_and_gain(1)
         add_residual(2)
         square(2)
         add_residual(3)
         root(2)
-        centre_and_gain(1)
-        square(3)
         invert(1)
+        square(3)
         centre_and_gain(2)
         root(3)
         finish(1, 1)
         invert(2)
         centre_and_gain(3)
-        finish(2, 1)
         invert(3)
+        finish(2, 1)
         finish(3, 2)

from contextlib import ExitStack

import concourse.mybir as mybir
from concourse.masks import make_identity

F32 = mybir.dt.float32
BF16 = mybir.dt.bfloat16
I32 = mybir.dt.int32
U32 = mybir.dt.uint32
U8 = mybir.dt.uint8
FP8X4 = mybir.dt.float8_e4m3fn_x4
FP4X4 = mybir.dt.float4_e2m1fn_x4
ALU = mybir.AluOpType
ACT = mybir.ActivationFunctionType

P = 128
HEADS = 8
HALF = 64
SENTENCES = 4
STRIPES = SENTENCES
K = HEADS * HALF
D_CONTENT = 384
D_MODEL = 512
COLUMN_GROUPS = ((0, 256), (256, 128), (384, 128))
VECTOR_ROWS = D_MODEL // P
EPS = 1e-3
ROOT_SCALE = 1.0 / (D_MODEL * D_MODEL * (D_MODEL - 1))

FLOPS = 2 * SENTENCES * P * K * D_MODEL


def load_scale_rows(nc, plane, scale_rows, quarters):
    for a in quarters:
        nc.sync.dma_start(
            out=plane[32 * a : 32 * a + 4, :].bitcast(I32),
            in_=scale_rows[4 * a : 4 * a + 4, :].bitcast(I32),
        )


def tile_multiheadattention_pa_s_kernel(
    tc,
    attn_out,
    inp,
    w_proj1_words,
    w_proj1_scales,
    w_proj2_words,
    w_proj2_scales,
    ln_a,
    ln_b,
    out,
):
    nc = tc.nc
    with ExitStack() as ctx:
        const = ctx.enter_context(tc.tile_pool(name="const", bufs=1))
        feature_pool = ctx.enter_context(tc.tile_pool(name="features", bufs=2 * SENTENCES))
        operand_pool = ctx.enter_context(tc.tile_pool(name="operands", bufs=2 * SENTENCES))
        row_pool = ctx.enter_context(tc.tile_pool(name="rows", bufs=SENTENCES))
        stat_pool = ctx.enter_context(tc.tile_pool(name="stats", bufs=2 * SENTENCES))
        transposed_pool = ctx.enter_context(tc.psum_pool(name="transposed", bufs=3))
        product_pool = ctx.enter_context(tc.psum_pool(name="product", bufs=3))
        spread_pool = ctx.enter_context(tc.psum_pool(name="spread", bufs=1))
        ctx.enter_context(tc.manual_schedule())

        w_words = const.tile([P, 2 * D_MODEL], U8, align_bytes=512)
        w_scales = const.tile([P, D_MODEL], U8, align_bytes=512)
        nc.gpsimd.memset(w_scales[:].bitcast(F32), 0.0)
        vector_rows = const.tile([P, P], BF16, align_bytes=512)
        nc.vector.memset(vector_rows[:], 0.0)
        nc.scalar.dma_start(out=vector_rows[0:VECTOR_ROWS, :], in_=ln_a.rearrange("(r c) -> r c", c=P))
        nc.scalar.dma_start(
            out=vector_rows[VECTOR_ROWS : 2 * VECTOR_ROWS, :], in_=ln_b.rearrange("(r c) -> r c", c=P)
        )

        features = {}
        raw_features = {}
        residual = const.tile([P, SENTENCES, D_MODEL], BF16, align_bytes=512)

        attn_stripes = attn_out.rearrange("h b l f -> h (b l) f").rearrange("h (p s) f -> p h s f", s=STRIPES)
        inp_stripes = inp.rearrange("(p s) d -> p s d", s=STRIPES)
        out_stripes = out.rearrange("(p s) d -> p s d", s=STRIPES)

        def load_half(s, half):
            x = feature_pool.tile([P, HEADS, HALF], BF16, align_bytes=512)
            nc.sync.dma_start(out=x[:], in_=attn_stripes[:, :, s, half * HALF : (half + 1) * HALF])
            features[(s, half)] = x

        def load_whole(first, last):
            raw = const.tile([P, HEADS, last - first, 2 * HALF], BF16, name=f"raw_{first}", align_bytes=512)
            nc.sync.dma_start(out=raw[:], in_=attn_stripes[:, :, first:last, :])
            for s in range(first, last):
                raw_features[s] = raw[:, :, s - first, :]

        def load_residual(first, last):
            nc.gpsimd.dma_start(out=residual[:, first:last, :], in_=inp_stripes[:, first:last, :])

        load_half(0, 0)
        load_half(0, 1)
        load_scale_rows(nc, w_scales[:, :D_CONTENT], w_proj1_scales[0], range(3))
        load_whole(1, 2)
        load_scale_rows(nc, w_scales[:, :D_CONTENT], w_proj1_scales[0], range(3, 4))
        nc.sync.dma_start(out=w_words[:, : 2 * D_CONTENT].bitcast(I32), in_=w_proj1_words[0].bitcast(I32))
        nc.sync.dma_start(out=w_words[:, 2 * D_CONTENT :].bitcast(I32), in_=w_proj2_words[0].bitcast(I32))
        load_scale_rows(nc, w_scales[:, D_CONTENT:], w_proj2_scales[0], range(4))
        for s in (2, 3):
            load_half(s, 0)
            load_half(s, 1)

        identity = const.tile([P, P], F32)
        make_identity(nc, identity[:])
        load_residual(0, 2)
        load_residual(2, 4)

        one = const.tile([P, SENTENCES], F32)
        nc.vector.memset(one[:], 1.0)
        root_of_one = const.tile([P, 1], F32)
        nc.scalar.activation(out=root_of_one[:], in_=one[:, 0:1], func=ACT.Sqrt)
        under_root = const.tile([P, 2, SENTENCES], F32)
        nc.vector.tensor_scalar(
            out=under_root[:, 1, :], in0=one[:], scalar1=EPS * EPS / ROOT_SCALE, scalar2=None, op0=ALU.mult
        )

        vector_rows_f32 = const.tile([P, P], F32)
        nc.vector.tensor_copy(out=vector_rows_f32[:], in_=vector_rows[:])
        vector_columns = const.tile([P, 2 * VECTOR_ROWS], F32)

        def turn_vector_rows():
            transposed = transposed_pool.tile([P, 2, P], F32)
            nc.tensor.transpose(transposed[:, 0, :], vector_rows_f32[:], identity[:])
            nc.vector.tensor_copy(out=vector_columns[:], in_=transposed[:, 0, : 2 * VECTOR_ROWS])

        gain = spread_pool.tile([P, D_MODEL], F32)
        bias = spread_pool.tile([P, D_MODEL], F32)

        def spread(vector, first_column):
            for r in range(VECTOR_ROWS):
                column = vector_columns[:, first_column + r : first_column + r + 1]
                nc.tensor.transpose(vector[:, r * P : (r + 1) * P], column.to_broadcast([P, P]), identity[:])

        sorted_words = {}
        transposed_words = {}
        grouped_values = {}
        operands = {}
        products = {}
        rows = {}
        means = {}
        sums = {}
        sigmas = {}
        centred_rows = {}

        def sort(s, half):
            words = raw_features[s][:, :, half * HALF : (half + 1) * HALF].bitcast(F32)
            x = feature_pool.tile([P, 2, HEADS, HALF // 4], F32, name="sorted_words", align_bytes=512)
            nc.vector.tensor_copy(out=x[:], in_=words.rearrange("l h (i u) -> l u h i", u=2))
            sorted_words[(s, half)] = x

        def turn(s, half):
            transposed = transposed_pool.tile([P, 2, P], F32)
            for u in range(2):
                if (s, half) in features:
                    words = features[(s, half)][:].rearrange("l h j -> l (h j)").bitcast(F32)[:, u : K // 2 : 2]
                else:
                    words = sorted_words[(s, half)][:, u, :, :].rearrange("l h i -> l (h i)")
                nc.tensor.transpose(transposed[:, u, :], words, identity[:])
            transposed_words[(s, half)] = transposed

        def group(b, half):
            grouped = operand_pool.tile([P, P, 4], BF16, align_bytes=512)
            nc.scalar.copy(
                out=grouped[:].bitcast(F32), in_=transposed_words[(b, half)][:].rearrange("p u l -> p l u")
            )
            grouped_values[(b, half)] = grouped

        def quantize(b, half):
            codes = operand_pool.tile([P, P], U32, align_bytes=512)
            scales = operand_pool.tile([P, P], U8, align_bytes=512)
            nc.vector.quantize_mx(
                out=codes[:].bitcast(FP8X4),
                scales=scales[:],
                in_=grouped_values[(b, half)][:].rearrange("p l t -> p (l t)"),
            )
            operands[(b, half)] = (codes, scales)

        def multiply(b):
            z_psum = product_pool.tile([P, D_MODEL], F32)
            for n, width in COLUMN_GROUPS:
                codes, scales = operands[(b, 0 if n < D_CONTENT else 1)]
                nc.tensor.matmul_mx(
                    out=z_psum[:, n : n + width],
                    lhsT=codes[:].bitcast(FP8X4),
                    lhsT_scale=scales[:],
                    rhs=w_words[:, 2 * n : 2 * (n + width)].bitcast(FP4X4),
                    rhs_scale=w_scales[:, n : n + width],
                    start=True,
                    stop=True,
                )
            products[b] = z_psum

        def add_residual(b):
            z = row_pool.tile([P, D_MODEL], F32, align_bytes=512)
            row_sum = stat_pool.tile([P, 1], F32)
            nc.vector.scalar_tensor_tensor(
                out=z[:],
                in0=products[b][:],
                scalar=1.0,
                in1=residual[:, b, :],
                op0=ALU.mult,
                op1=ALU.add,
                accum_out=row_sum[:],
            )
            rows[b] = z
            sums[b] = row_sum
            neg_mean = stat_pool.tile([P, 1], F32)
            nc.gpsimd.tensor_scalar(
                out=neg_mean[:], in0=row_sum[:], scalar1=-1.0 / D_MODEL, scalar2=0.0, op0=ALU.mult, op1=ALU.add
            )
            means[b] = neg_mean

        def square(b):
            squares = row_pool.tile([P, D_MODEL], BF16, align_bytes=512)
            nc.scalar.activation(
                out=squares[:],
                in_=rows[b][:],
                func=ACT.Square,
                bias=sums[b][:],
                scale=-float(D_MODEL),
                accum_out=under_root[:, 0, b : b + 1],
            )

        def root(b):
            roots = stat_pool.tile([P, 2], F32)
            sigma_eps = stat_pool.tile([P, 1], F32)
            nc.scalar.activation(
                out=roots[:], in_=under_root[:, :, b], func=ACT.Sqrt, scale=ROOT_SCALE, accum_out=sigma_eps[:]
            )
            sigmas[b] = sigma_eps

        def centre_and_gain(b):
            centred = row_pool.tile([P, D_MODEL], F32, align_bytes=512)
            nc.vector.scalar_tensor_tensor(
                out=centred[:], in0=rows[b][:], scalar=means[b][:], in1=gain[:], op0=ALU.add, op1=ALU.mult
            )
            centred_rows[b] = centred

        inverses = {}

        def invert(b):
            inverse = stat_pool.tile([P, 1], F32)
            nc.vector.reciprocal(out=inverse[:], in_=sigmas[b][:])
            inverses[b] = inverse

        def finish(b, pieces):
            result = row_pool.tile([P, D_MODEL], F32, align_bytes=512)
            width = D_MODEL // pieces
            for n in range(0, D_MODEL, width):
                nc.vector.scalar_tensor_tensor(
                    out=result[:, n : n + width],
                    in0=centred_rows[b][:, n : n + width],
                    scalar=inverses[b][:],
                    in1=bias[:, n : n + width],
                    op0=ALU.mult,
                    op1=ALU.add,
                )
                nc.sync.dma_start(out=out_stripes[:, b, n : n + width], in_=result[:, n : n + width])

        turn(0, 0)
        group(0, 0)
        turn(0, 1)
        group(0, 1)
        turn_vector_rows()
        quantize(0, 0)
        quantize(0, 1)
        sort(1, 0)
        sort(1, 1)
        spread(gain, 0)
        turn(1, 0)
        group(1, 0)
        turn(1, 1)
        group(1, 1)
        multiply(0)
        add_residual(0)
        spread(bias, VECTOR_ROWS)
        quantize(1, 0)
        quantize(1, 1)
        multiply(1)
        square(0)
        root(0)
        centre_and_gain(0)
        turn(2, 0)
        group(2, 0)
        turn(2, 1)
        group(2, 1)
        add_residual(1)
        turn(3, 0)
        group(3, 0)
        turn(3, 1)
        group(3, 1)
        invert(0)
        quantize(2, 0)
        finish(0, 1)
        quantize(2, 1)
        multiply(2)
        square(1)
        quantize(3, 0)
        quantize(3, 1)
        multiply(3)
        root(1)
        centre_and_gain(1)
        add_residual(2)
        square(2)
        add_residual(3)
        root(2)
        invert(1)
        square(3)
        centre_and_gain(2)
        root(3)
        finish(1, 1)
        invert(2)
        centre_and_gain(3)
        invert(3)
        finish(2, 1)
        finish(3, 2)
